import numpy as np
import ml_dtypes


def mxq(x, axis, fmt="e4m3"):
    dtype, down = {"e4m3": (ml_dtypes.float8_e4m3fn, 7), "e5m2": (ml_dtypes.float8_e5m2, 14)}[fmt]
    v = np.moveaxis(np.asarray(x, np.float32).astype(ml_dtypes.bfloat16).astype(np.float64), axis, -1)
    blocks = v.reshape(v.shape[:-1] + (-1, 32))
    amax = np.abs(blocks).max(-1, keepdims=True)
    byte = np.maximum(np.where(amax > 0, np.frexp(amax)[1] - 1 + 127, 0) - down, 1)
    scale = np.exp2(byte - 127.0)
    codes = (blocks / scale).astype(np.float32).astype(dtype).astype(np.float64)
    return np.moveaxis((codes * scale).reshape(v.shape), -1, axis)


WIDE = False


def mx_kscale(k):
    if not WIDE:
        return np.ones(k)
    levels = np.array([10, -10, 5, -5, 0])
    a = np.random.permutation(np.resize(levels, k // 512 * 4)).reshape(k // 512, 4)
    idx = np.arange(k)
    return np.exp2(a[idx // 512, idx % 128 // 32])


BF16 = ml_dtypes.bfloat16


def bf(x):
    return np.asarray(x, np.float32).astype(BF16)


def f64(x):
    return np.asarray(x).astype(np.float64)


B, G, DB, DR = 128, 16, 1024, 2048


def mish(v):
    return v * np.tanh(np.log(1.0 + np.exp(v)))


def setup_inputs():
    s, t = mx_kscale(DR), mx_kscale(DB)
    return {"BB_feature": bf(np.random.standard_normal((B, G, DB)) * t),
            "RF_feature": bf(np.random.standard_normal((B, DR)) * s),
            "W_bbbb": bf(np.random.standard_normal((DB, DB)) / np.sqrt(DB) / t),
            "b_bbbb": bf(np.random.standard_normal(DB) * 0.5),
            "W_rfbb": bf(np.random.standard_normal((DB, DR)) / np.sqrt(DR) / s),
            "b_rfbb": bf(np.random.standard_normal(DB) * 0.5)}


def reference(BB_feature, RF_feature, W_bbbb, b_bbbb, W_rfbb, b_rfbb):
    RF_to_BB = mish((mxq(f64(RF_feature), 1, "e4m3") @ mxq(f64(W_rfbb), 1, "e4m3").T) + f64(b_rfbb))
    BB_to_BB = mish((mxq(f64(BB_feature), 2, "e4m3") @ mxq(f64(W_bbbb), 1, "e4m3").T) + f64(b_bbbb))
    return BB_to_BB + RF_to_BB[:, None, :]

@@ -1,0 +1,245 @@
+from contextlib import ExitStack
+
+import concourse.mybir as mybir
+from concourse.masks import make_identity
+
+F32 = mybir.dt.float32
+BF16 = mybir.dt.bfloat16
+U32 = mybir.dt.uint32
+U8 = mybir.dt.uint8
+FP8X4 = mybir.dt.float8_e4m3fn_x4
+FUNC = mybir.ActivationFunctionType
+ALU = mybir.AluOpType
+
+P = 128
+GROUPS = 16
+D_BB = 1024
+D_RF = 2048
+K_PASS = 512
+HALF = 512
+BATCH = 4096
+CHUNK = 4
+BLOCKS_PER_BANK = 4
+TINY = 2.0 ** -60
+
+FLOPS = 2 * P * GROUPS * D_BB * D_BB + 2 * P * D_RF * D_BB
+
+
+def tile_gnn_layer_pb_kernel(tc, BB_feature, RF_feature, W_bbbb, b_bbbb, W_rfbb, b_rfbb, out):
+    nc = tc.nc
+    with ExitStack() as stack:
+        const = stack.enter_context(tc.tile_pool(name="const", bufs=1))
+        raw_pool = stack.enter_context(tc.tile_pool(name="raw", bufs=4))
+        grouped_pool = stack.enter_context(tc.tile_pool(name="grouped", bufs=3))
+        keep = stack.enter_context(tc.tile_pool(name="keep", bufs=1))
+        turn = stack.enter_context(tc.tile_pool(name="turn", bufs=3))
+        work = stack.enter_context(tc.tile_pool(name="work", bufs=1))
+        flip_psum = stack.enter_context(tc.psum_pool(name="flip", bufs=4))
+        acc_psum = stack.enter_context(tc.psum_pool(name="acc", bufs=4))
+        stack.enter_context(tc.manual_schedule())
+
+        ident = const.tile([P, P], F32, name="ident")
+        make_identity(nc, ident[:])
+        tiny = const.tile([P, 1], F32, name="tiny")
+        nc.vector.memset(tiny[:], TINY)
+        warm = const.tile([P, 1], F32, name="warm")
+        bias_bb = const.tile([P, D_BB], BF16, name="bias_bb")
+        bias_rf = const.tile([P, D_BB], BF16, name="bias_rf")
+        nc.scalar.dma_start(out=bias_bb[:], in_=b_bbbb.partition_broadcast(P))
+        nc.scalar.dma_start(out=bias_rf[:], in_=b_rfbb.partition_broadcast(P))
+
+        def load_sigmoid_table():
+            nc.scalar.activation(out=warm[:], in_=tiny[:], func=FUNC.Sigmoid)
+
+        load_sigmoid_table()
+
+        z = [work.tile([P, D_BB], F32, name="z%d" % g) for g in range(GROUPS + 1)]
+        w = [work.tile([P, D_BB], F32, name="w%d" % g) for g in range(GROUPS + 1)]
+        RF = GROUPS
+
+        def load(view, row_tiles):
+            raw = raw_pool.tile([P, BATCH], BF16, name="raw")
+            cols = view.shape[-1] * row_tiles
+            nc.sync.dma_start(out=raw[:, :cols].rearrange("p (j k) -> p j k", j=row_tiles), in_=view)
+            return raw
+
+        def flip(raw, blocks):
+            words = raw[:].bitcast(F32)
+            banks = []
+            for first in range(0, blocks, BLOCKS_PER_BANK):
+                bank = flip_psum.tile([P, BLOCKS_PER_BANK, P], F32, name="bank")
+                for s in range(BLOCKS_PER_BANK):
+                    n = first + s
+                    nc.tensor.transpose(bank[:, s, :], words[:, n * P : (n + 1) * P], ident[:])
+                banks.append(bank)
+            return banks
+
+        def regroup(banks, passes, row_tiles, scalar_banks):
+            grouped = grouped_pool.tile([P, BATCH], BF16, name="grouped", align_bytes=64)
+            cols = passes * row_tiles * P * 4
+            pairs = grouped[:, :cols].bitcast(F32).rearrange(
+                "p (c j r u) -> p c j r u", c=passes, j=row_tiles, u=2
+            )
+            banks_per_row_tile = passes // 2
+            for k, bank in enumerate(banks):
+                j, h = divmod(k, banks_per_row_tile)
+                dst = pairs[:, 2 * h : 2 * h + 2, j]
+                src = bank[:].rearrange("p (c u) r -> p c r u", u=2)
+                if k >= len(banks) - scalar_banks:
+                    nc.scalar.copy(out=dst, in_=src)
+                else:
+                    nc.vector.tensor_copy(out=dst, in_=src)
+            return grouped[:, :cols]
+
+        def quantise(grouped, pool, tag):
+            words = grouped.shape[-1] // 4
+            codes = pool.tile([P, words], U32, name="codes_" + tag, align_bytes=64)
+            scales = pool.tile([P, words], U8, name="scales_" + tag, align_bytes=64)
+            nc.vector.quantize_mx(out=codes[:].bitcast(FP8X4), scales=scales[:], in_=grouped)
+            return codes, scales
+
+        def product(acc, stationary, j, row_tiles, moving, width, passes):
+            s_codes, s_scales = stationary
+            m_codes, m_scales = moving
+            for c in range(passes):
+                s_cols = slice((c * row_tiles + j) * P, (c * row_tiles + j + 1) * P)
+                m_cols = slice(c * width, (c + 1) * width)
+                nc.tensor.matmul_mx(
+                    out=acc,
+                    lhsT=s_codes[:, s_cols].bitcast(FP8X4),
+                    lhsT_scale=s_scales[:, s_cols],
+                    rhs=m_codes[:, m_cols].bitcast(FP8X4),
+                    rhs_scale=m_scales[:, m_cols],
+                    start=(c == 0),
+                    stop=(c == passes - 1),
+                )
+
+        def x_view(q):
+            return BB_feature[:, q * CHUNK : (q + 1) * CHUNK, :]
+
+        def w_view(weight, first_row, row_tiles):
+            return weight[first_row : first_row + row_tiles * P, :].rearrange("(j p) k -> p j k", p=P)
+
+        w_bb = [None, None]
+
+        def multiply_bb(x_mx, g, h):
+            acc = acc_psum.tile([P, HALF], F32, name="acc")
+            product(acc[:], x_mx, g % CHUNK, CHUNK, w_bb[h], HALF, D_BB // K_PASS)
+            cols = slice(h * HALF, (h + 1) * HALF)
+            nc.vector.tensor_tensor(out=z[g][:, cols], in0=acc[:], in1=bias_bb[:, cols], op=ALU.add)
+
+        def sigmoid(g, cols=slice(0, D_BB)):
+            nc.scalar.activation(out=w[g][:, cols], in_=z[g][:, cols], func=FUNC.Sigmoid, scale=-1.0)
+
+        def log(g):
+            nc.scalar.activation(out=w[g][:], in_=w[g][:], func=FUNC.Ln, bias=tiny[:])
+
+        def tanh(g):
+            nc.scalar.activation(out=w[g][:], in_=w[g][:], func=FUNC.Tanh, scale=-1.0)
+
+        def times_z(engine, g):
+            engine.tensor_tensor(out=w[g][:], in0=z[g][:], in1=w[g][:], op=ALU.mult)
+
+        def finish(g):
+            nc.vector.tensor_tensor(out=w[g][:], in0=w[g][:], in1=w[RF][:], op=ALU.add)
+            nc.sync.dma_start(out=out[:, g, :], in_=w[g][:])
+
+        raw_wbb0 = load(w_view(W_bbbb, 0, 4), 4)
+        raw_x0 = load(x_view(0), CHUNK)
+        raw_wbb1 = load(w_view(W_bbbb, HALF, 4), 4)
+        raw_x1 = load(x_view(1), CHUNK)
+
+        g_wbb0 = regroup(flip(raw_wbb0, 16), 2, 4, 2)
+        raw_x2 = load(x_view(2), CHUNK)
+        w_bb[0] = quantise(g_wbb0, keep, "wbb0")
+        g_x0 = regroup(flip(raw_x0, 16), 2, CHUNK, 2)
+        raw_rf = load(RF_feature.rearrange("b (j k) -> b j k", j=1), 1)
+        x0 = quantise(g_x0, turn, "turn")
+        g_wbb1 = regroup(flip(raw_wbb1, 16), 2, 4, 4)
+        raw_wrf = [load(w_view(W_rfbb, 0, 2), 2)]
+        for g in range(0, CHUNK // 2):
+            multiply_bb(x0, g, 0)
+            sigmoid(g, slice(0, HALF))
+        w_bb[1] = quantise(g_wbb1, keep, "wbb1")
+        for g in range(CHUNK // 2, CHUNK):
+            multiply_bb(x0, g, 0)
+            sigmoid(g, slice(0, HALF))
+        banks_x1 = flip(raw_x1, 16)
+        raw_wrf.append(load(w_view(W_rfbb, 2 * P, 2), 2))
+        for g in range(0, CHUNK):
+            multiply_bb(x0, g, 1)
+            sigmoid(g, slice(HALF, D_BB))
+        g_x1 = regroup(banks_x1, 2, CHUNK, 0)
+        for g in range(0, CHUNK):
+            log(g)
+        banks_x2 = flip(raw_x2, 16)
+        x1 = quantise(g_x1, turn, "turn")
+        g_x2 = regroup(banks_x2, 2, CHUNK, 0)
+        raw_wrf.append(load(w_view(W_rfbb, 4 * P, 2), 2))
+        for g in range(CHUNK, 2 * CHUNK):
+            multiply_bb(x1, g, 0)
+            multiply_bb(x1, g, 1)
+            sigmoid(g)
+        x2 = quantise(g_x2, turn, "turn")
+        for g in range(0, CHUNK):
+            tanh(g)
+            times_z(nc.gpsimd, g)
+        for g in range(CHUNK, 2 * CHUNK):
+            log(g)
+
+        g_rf = regroup(flip(raw_rf, 8), 4, 1, 0)
+        raw_wrf.append(load(w_view(W_rfbb, 6 * P, 2), 2))
+        g_wrf = regroup(flip(raw_wrf[0], 16), 4, 2, 0)
+        raw_x3 = load(x_view(3), CHUNK)
+        for g in range(2 * CHUNK, 3 * CHUNK):
+            multiply_bb(x2, g, 0)
+            multiply_bb(x2, g, 1)
+            sigmoid(g)
+        rf_mx = quantise(g_rf, keep, "rf")
+        wrf_mx = quantise(g_wrf, turn, "turn")
+        for g in range(CHUNK, 2 * CHUNK):
+            tanh(g)
+            times_z(nc.gpsimd, g)
+
+        WIDTH_RF = 2 * P
+        for i in range(4):
+            if i < 3:
+                g_next = regroup(flip(raw_wrf[i + 1], 16), 4, 2, 0)
+            else:
+                g_next = regroup(flip(raw_x3, 16), 2, CHUNK, 0)
+            acc = acc_psum.tile([P, HALF], F32, name="acc")
+            product(acc[:, :WIDTH_RF], rf_mx, 0, 1, wrf_mx, WIDTH_RF, D_RF // K_PASS)
+            cols = slice(i * WIDTH_RF, (i + 1) * WIDTH_RF)
+            nc.vector.tensor_tensor(out=z[RF][:, cols], in0=acc[:, :WIDTH_RF], in1=bias_rf[:, cols], op=ALU.add)
+            wrf_mx = quantise(g_next, turn, "turn")
+        x3 = wrf_mx
+        sigmoid(RF)
+
+        log(RF)
+        for g in range(2 * CHUNK, 3 * CHUNK):
+            log(g)
+        for g in range(3 * CHUNK, GROUPS):
+            multiply_bb(x3, g, 0)
+            multiply_bb(x3, g, 1)
+
+        load_sigmoid_table()
+        tanh(RF)
+        times_z(nc.vector, RF)
+        for g in range(0, 2 * CHUNK):
+            finish(g)
+        for g in range(3 * CHUNK, GROUPS):
+            sigmoid(g)
+
+        def last_steps(first):
+            for g in range(first, first + CHUNK, 2):
+                tanh(g)
+                times_z(nc.gpsimd, g)
+                tanh(g + 1)
+                times_z(nc.vector, g + 1)
+                finish(g + 1)
+                finish(g)
+
+        last_steps(2 * CHUNK)
+        for g in range(3 * CHUNK, GROUPS):
+            log(g)
+        last_steps(3 * CHUNK)

@@ -38,30 +38,54 @@ def tile_gnn_layer_pb_kernel(tc, BB_feature, RF_feature, W_bbbb, b_bbbb, W_rfbb,
         acc_psum = stack.enter_context(tc.psum_pool(name="acc", bufs=4))
         stack.enter_context(tc.manual_schedule())
 
+        def load(view, row_tiles):
+            raw = raw_pool.tile([P, BATCH], BF16, name="raw")
+            cols = view.shape[-1] * row_tiles
+            nc.sync.dma_start(out=raw[:, :cols].rearrange("p (j k) -> p j k", j=row_tiles), in_=view)
+            return raw
+
+        def x_view(q):
+            return BB_feature[:, q * CHUNK : (q + 1) * CHUNK, :]
+
+        def w_view(weight, first_row, row_tiles):
+            return weight[first_row : first_row + row_tiles * P, :].rearrange("(j p) k -> p j k", p=P)
+
+        raw_wbb0 = load(w_view(W_bbbb, 0, 4), 4)
+        bias_rows = const.tile([P, 2 * D_BB], BF16, name="bias_rows")
+        nc.vector.memset(bias_rows[:], 0.0)
+        nc.sync.dma_start(out=bias_rows[0:1, :D_BB], in_=b_bbbb.rearrange("(o n) -> o n", o=1))
+        nc.sync.dma_start(out=bias_rows[0:1, D_BB:], in_=b_rfbb.rearrange("(o n) -> o n", o=1))
+        raw_x0 = load(x_view(0), CHUNK)
+        raw_wbb1 = load(w_view(W_bbbb, HALF, 4), 4)
+        raw_x1 = load(x_view(1), CHUNK)
+
         ident = const.tile([P, P], F32, name="ident")
         make_identity(nc, ident[:])
         tiny = const.tile([P, 1], F32, name="tiny")
         nc.vector.memset(tiny[:], TINY)
         warm = const.tile([P, 1], F32, name="warm")
+
+        ones = const.tile([P, P], BF16, name="ones")
+        nc.vector.memset(ones[:], 1.0)
         bias_bb = const.tile([P, D_BB], BF16, name="bias_bb")
         bias_rf = const.tile([P, D_BB], BF16, name="bias_rf")
-        nc.scalar.dma_start(out=bias_bb[:], in_=b_bbbb.partition_broadcast(P))
-        nc.scalar.dma_start(out=bias_rf[:], in_=b_rfbb.partition_broadcast(P))
 
         def load_sigmoid_table():
             nc.scalar.activation(out=warm[:], in_=tiny[:], func=FUNC.Sigmoid)
 
         load_sigmoid_table()
 
+        def spread_biases():
+            for spread, first in ((bias_bb, 0), (bias_rf, D_BB)):
+                for h in range(D_BB // HALF):
+                    row = bias_rows[:, first + h * HALF : first + (h + 1) * HALF]
+                    acc = acc_psum.tile([P, HALF], F32, name="acc")
+                    nc.tensor.matmul(out=acc[:], lhsT=ones[:], rhs=row, start=True, stop=True)
+                    nc.scalar.copy(out=spread[:, h * HALF : (h + 1) * HALF], in_=acc[:])
+
         z = [work.tile([P, D_BB], F32, name="z%d" % g) for g in range(GROUPS + 1)]
         w = [work.tile([P, D_BB], F32, name="w%d" % g) for g in range(GROUPS + 1)]
         RF = GROUPS
-
-        def load(view, row_tiles):
-            raw = raw_pool.tile([P, BATCH], BF16, name="raw")
-            cols = view.shape[-1] * row_tiles
-            nc.sync.dma_start(out=raw[:, :cols].rearrange("p (j k) -> p j k", j=row_tiles), in_=view)
-            return raw
 
         def flip(raw, blocks):
             words = raw[:].bitcast(F32)
@@ -114,12 +138,6 @@ def tile_gnn_layer_pb_kernel(tc, BB_feature, RF_feature, W_bbbb, b_bbbb, W_rfbb,
                     stop=(c == passes - 1),
                 )
 
-        def x_view(q):
-            return BB_feature[:, q * CHUNK : (q + 1) * CHUNK, :]
-
-        def w_view(weight, first_row, row_tiles):
-            return weight[first_row : first_row + row_tiles * P, :].rearrange("(j p) k -> p j k", p=P)
-
         w_bb = [None, None]
 
         def multiply_bb(x_mx, g, h):
@@ -144,12 +162,8 @@ def tile_gnn_layer_pb_kernel(tc, BB_feature, RF_feature, W_bbbb, b_bbbb, W_rfbb,
             nc.vector.tensor_tensor(out=w[g][:], in0=w[g][:], in1=w[RF][:], op=ALU.add)
             nc.sync.dma_start(out=out[:, g, :], in_=w[g][:])
 
-        raw_wbb0 = load(w_view(W_bbbb, 0, 4), 4)
-        raw_x0 = load(x_view(0), CHUNK)
-        raw_wbb1 = load(w_view(W_bbbb, HALF, 4), 4)
-        raw_x1 = load(x_view(1), CHUNK)
-
         g_wbb0 = regroup(flip(raw_wbb0, 16), 2, 4, 2)
+        spread_biases()
         raw_x2 = load(x_view(2), CHUNK)
         w_bb[0] = quantise(g_wbb0, keep, "wbb0")
         g_x0 = regroup(flip(raw_x0, 16), 2, CHUNK, 2)
@@ -205,15 +219,14 @@ def tile_gnn_layer_pb_kernel(tc, BB_feature, RF_feature, W_bbbb, b_bbbb, W_rfbb,
         for i in range(4):
             if i < 3:
                 g_next = regroup(flip(raw_wrf[i + 1], 16), 4, 2, 0)
-            else:
-                g_next = regroup(flip(raw_x3, 16), 2, CHUNK, 0)
             acc = acc_psum.tile([P, HALF], F32, name="acc")
             product(acc[:, :WIDTH_RF], rf_mx, 0, 1, wrf_mx, WIDTH_RF, D_RF // K_PASS)
             cols = slice(i * WIDTH_RF, (i + 1) * WIDTH_RF)
             nc.vector.tensor_tensor(out=z[RF][:, cols], in0=acc[:, :WIDTH_RF], in1=bias_rf[:, cols], op=ALU.add)
-            wrf_mx = quantise(g_next, turn, "turn")
-        x3 = wrf_mx
+            if i < 3:
+                wrf_mx = quantise(g_next, turn, "turn")
         sigmoid(RF)
+        x3 = quantise(regroup(flip(raw_x3, 16), 2, CHUNK, 0), turn, "turn")
 
         log(RF)
         for g in range(2 * CHUNK, 3 * CHUNK):

@@ -158,8 +158,18 @@ def tile_gnn_layer_pb_kernel(tc, BB_feature, RF_feature, W_bbbb, b_bbbb, W_rfbb,
         def times_z(engine, g):
             engine.tensor_tensor(out=w[g][:], in0=z[g][:], in1=w[g][:], op=ALU.mult)
 
+        rf_banks = []
+
+        def park_rf_in_psum():
+            for h in range(D_BB // HALF):
+                bank = flip_psum.tile([P, HALF], F32, name="bank")
+                nc.tensor.matmul(out=bank[:], lhsT=ident[:], rhs=w[RF][:, h * HALF : (h + 1) * HALF], start=True, stop=True)
+                rf_banks.append(bank)
+
         def finish(g):
-            nc.vector.tensor_tensor(out=w[g][:], in0=w[g][:], in1=w[RF][:], op=ALU.add)
+            for h in range(D_BB // HALF):
+                cols = slice(h * HALF, (h + 1) * HALF)
+                nc.vector.tensor_tensor(out=w[g][:, cols], in0=rf_banks[h][:], in1=w[g][:, cols], op=ALU.add)
             nc.sync.dma_start(out=out[:, g, :], in_=w[g][:])
 
         g_wbb0 = regroup(flip(raw_wbb0, 16), 2, 4, 2)
@@ -238,21 +248,22 @@ def tile_gnn_layer_pb_kernel(tc, BB_feature, RF_feature, W_bbbb, b_bbbb, W_rfbb,
         load_sigmoid_table()
         tanh(RF)
         times_z(nc.vector, RF)
+        park_rf_in_psum()
         for g in range(0, 2 * CHUNK):
             finish(g)
         for g in range(3 * CHUNK, GROUPS):
             sigmoid(g)
 
-        def last_steps(first):
-            for g in range(first, first + CHUNK, 2):
-                tanh(g)
-                times_z(nc.gpsimd, g)
-                tanh(g + 1)
-                times_z(nc.vector, g + 1)
-                finish(g + 1)
-                finish(g)
-
-        last_steps(2 * CHUNK)
+        for g in range(2 * CHUNK, 3 * CHUNK):
+            tanh(g)
+            times_z(nc.gpsimd, g)
+            finish(g)
         for g in range(3 * CHUNK, GROUPS):
             log(g)
-        last_steps(3 * CHUNK)
+        for g in range(3 * CHUNK, GROUPS, 2):
+            tanh(g)
+            times_z(nc.gpsimd, g)
+            tanh(g + 1)
+            times_z(nc.vector, g + 1)
+            finish(g + 1)
+            finish(g)

@@ -51,11 +51,11 @@ def tile_gnn_layer_pb_kernel(tc, BB_feature, RF_feature, W_bbbb, b_bbbb, W_rfbb,
             return weight[first_row : first_row + row_tiles * P, :].rearrange("(j p) k -> p j k", p=P)
 
         raw_wbb0 = load(w_view(W_bbbb, 0, 4), 4)
+        raw_x0 = load(x_view(0), CHUNK)
         bias_rows = const.tile([P, 2 * D_BB], BF16, name="bias_rows")
         nc.vector.memset(bias_rows[:], 0.0)
         nc.sync.dma_start(out=bias_rows[0:1, :D_BB], in_=b_bbbb.rearrange("(o n) -> o n", o=1))
         nc.sync.dma_start(out=bias_rows[0:1, D_BB:], in_=b_rfbb.rearrange("(o n) -> o n", o=1))
-        raw_x0 = load(x_view(0), CHUNK)
         raw_wbb1 = load(w_view(W_bbbb, HALF, 4), 4)
         raw_x1 = load(x_view(1), CHUNK)
 
@@ -75,13 +75,12 @@ def tile_gnn_layer_pb_kernel(tc, BB_feature, RF_feature, W_bbbb, b_bbbb, W_rfbb,
 
         load_sigmoid_table()
 
-        def spread_biases():
-            for spread, first in ((bias_bb, 0), (bias_rf, D_BB)):
-                for h in range(D_BB // HALF):
-                    row = bias_rows[:, first + h * HALF : first + (h + 1) * HALF]
-                    acc = acc_psum.tile([P, HALF], F32, name="acc")
-                    nc.tensor.matmul(out=acc[:], lhsT=ones[:], rhs=row, start=True, stop=True)
-                    nc.scalar.copy(out=spread[:, h * HALF : (h + 1) * HALF], in_=acc[:])
+        def spread_bias(spread, first):
+            for h in range(D_BB // HALF):
+                row = bias_rows[:, first + h * HALF : first + (h + 1) * HALF]
+                acc = acc_psum.tile([P, HALF], F32, name="acc")
+                nc.tensor.matmul(out=acc[:], lhsT=ones[:], rhs=row, start=True, stop=True)
+                nc.vector.tensor_copy(out=spread[:, h * HALF : (h + 1) * HALF], in_=acc[:])
 
         z = [work.tile([P, D_BB], F32, name="z%d" % g) for g in range(GROUPS + 1)]
         w = [work.tile([P, D_BB], F32, name="w%d" % g) for g in range(GROUPS + 1)]
@@ -158,27 +157,30 @@ def tile_gnn_layer_pb_kernel(tc, BB_feature, RF_feature, W_bbbb, b_bbbb, W_rfbb,
         def times_z(engine, g):
             engine.tensor_tensor(out=w[g][:], in0=z[g][:], in1=w[g][:], op=ALU.mult)
 
-        rf_banks = []
-
-        def park_rf_in_psum():
+        def park(values, pool, name):
+            banks = []
             for h in range(D_BB // HALF):
-                bank = flip_psum.tile([P, HALF], F32, name="bank")
-                nc.tensor.matmul(out=bank[:], lhsT=ident[:], rhs=w[RF][:, h * HALF : (h + 1) * HALF], start=True, stop=True)
-                rf_banks.append(bank)
+                bank = pool.tile([P, HALF], F32, name=name)
+                nc.tensor.matmul(out=bank[:], lhsT=ident[:], rhs=values[:, h * HALF : (h + 1) * HALF], start=True, stop=True)
+                banks.append(bank)
+            return banks
 
-        def finish(g):
+        def with_parked(g, banks, op):
             for h in range(D_BB // HALF):
                 cols = slice(h * HALF, (h + 1) * HALF)
-                nc.vector.tensor_tensor(out=w[g][:, cols], in0=rf_banks[h][:], in1=w[g][:, cols], op=ALU.add)
+                nc.vector.tensor_tensor(out=w[g][:, cols], in0=banks[h][:], in1=w[g][:, cols], op=op)
+
+        def finish(g):
+            with_parked(g, rf_banks, ALU.add)
             nc.sync.dma_start(out=out[:, g, :], in_=w[g][:])
 
         g_wbb0 = regroup(flip(raw_wbb0, 16), 2, 4, 2)
-        spread_biases()
         raw_x2 = load(x_view(2), CHUNK)
         w_bb[0] = quantise(g_wbb0, keep, "wbb0")
         g_x0 = regroup(flip(raw_x0, 16), 2, CHUNK, 2)
         raw_rf = load(RF_feature.rearrange("b (j k) -> b j k", j=1), 1)
         x0 = quantise(g_x0, turn, "turn")
+        spread_bias(bias_bb, 0)
         g_wbb1 = regroup(flip(raw_wbb1, 16), 2, 4, 4)
         raw_wrf = [load(w_view(W_rfbb, 0, 2), 2)]
         for g in range(0, CHUNK // 2):
@@ -190,27 +192,24 @@ def tile_gnn_layer_pb_kernel(tc, BB_feature, RF_feature, W_bbbb, b_bbbb, W_rfbb,
             sigmoid(g, slice(0, HALF))
         banks_x1 = flip(raw_x1, 16)
         raw_wrf.append(load(w_view(W_rfbb, 2 * P, 2), 2))
+        g_x1 = regroup(banks_x1, 2, CHUNK, 4)
         for g in range(0, CHUNK):
             multiply_bb(x0, g, 1)
             sigmoid(g, slice(HALF, D_BB))
-        g_x1 = regroup(banks_x1, 2, CHUNK, 0)
-        for g in range(0, CHUNK):
-            log(g)
+
         banks_x2 = flip(raw_x2, 16)
         x1 = quantise(g_x1, turn, "turn")
-        g_x2 = regroup(banks_x2, 2, CHUNK, 0)
+        g_x2 = regroup(banks_x2, 2, CHUNK, 2)
         raw_wrf.append(load(w_view(W_rfbb, 4 * P, 2), 2))
         for g in range(CHUNK, 2 * CHUNK):
             multiply_bb(x1, g, 0)
             multiply_bb(x1, g, 1)
             sigmoid(g)
         x2 = quantise(g_x2, turn, "turn")
-        for g in range(0, CHUNK):
-            tanh(g)
-            times_z(nc.gpsimd, g)
-        for g in range(CHUNK, 2 * CHUNK):
+        for g in range(0, 2 * CHUNK):
             log(g)
 
+        spread_bias(bias_rf, D_BB)
         g_rf = regroup(flip(raw_rf, 8), 4, 1, 0)
         raw_wrf.append(load(w_view(W_rfbb, 6 * P, 2), 2))
         g_wrf = regroup(flip(raw_wrf[0], 16), 4, 2, 0)
@@ -221,7 +220,7 @@ def tile_gnn_layer_pb_kernel(tc, BB_feature, RF_feature, W_bbbb, b_bbbb, W_rfbb,
             sigmoid(g)
         rf_mx = quantise(g_rf, keep, "rf")
         wrf_mx = quantise(g_wrf, turn, "turn")
-        for g in range(CHUNK, 2 * CHUNK):
+        for g in range(0, 2 * CHUNK):
             tanh(g)
             times_z(nc.gpsimd, g)
 
@@ -236,6 +235,7 @@ def tile_gnn_layer_pb_kernel(tc, BB_feature, RF_feature, W_bbbb, b_bbbb, W_rfbb,
             if i < 3:
                 wrf_mx = quantise(g_next, turn, "turn")
         sigmoid(RF)
+        z_rf_banks = park(z[RF], flip_psum, "bank")
         x3 = quantise(regroup(flip(raw_x3, 16), 2, CHUNK, 0), turn, "turn")
 
         log(RF)
@@ -247,8 +247,8 @@ def tile_gnn_layer_pb_kernel(tc, BB_feature, RF_feature, W_bbbb, b_bbbb, W_rfbb,
 
         load_sigmoid_table()
         tanh(RF)
-        times_z(nc.vector, RF)
-        park_rf_in_psum()
+        with_parked(RF, z_rf_banks, ALU.mult)
+        rf_banks = park(w[RF], flip_psum, "bank")
         for g in range(0, 2 * CHUNK):
             finish(g)
         for g in range(3 * CHUNK, GROUPS):
@@ -260,10 +260,11 @@ def tile_gnn_layer_pb_kernel(tc, BB_feature, RF_feature, W_bbbb, b_bbbb, W_rfbb,
             finish(g)
         for g in range(3 * CHUNK, GROUPS):
             log(g)
+        z_banks = [park(z[g], acc_psum, "acc") for g in range(3 * CHUNK + 1, GROUPS, 2)]
         for g in range(3 * CHUNK, GROUPS, 2):
             tanh(g)
             times_z(nc.gpsimd, g)
             tanh(g + 1)
-            times_z(nc.vector, g + 1)
+            with_parked(g + 1, z_banks[(g - 3 * CHUNK) // 2], ALU.mult)
             finish(g + 1)
             finish(g)

@@ -15,11 +15,19 @@ P = 128
 GROUPS = 16
 D_BB = 1024
 D_RF = 2048
-K_PASS = 512
-HALF = 512
+PACK = 4
+K_PASS = P * PACK
+PASSES_BB = D_BB // K_PASS
+PASSES_RF = D_RF // K_PASS
+BANK = 512
+HALVES = D_BB // BANK
+BLOCKS_PER_BANK = BANK // P
+BLOCKS_PER_PASS = 2
 BATCH = 4096
-CHUNK = 4
-BLOCKS_PER_BANK = 4
+CHUNK = BATCH // D_BB
+TILES_W_RF = BATCH // D_RF
+BATCHES_W_RF = D_BB // (TILES_W_RF * P)
+RF = GROUPS
 TINY = 2.0 ** -60
 
 FLOPS = 2 * P * GROUPS * D_BB * D_BB + 2 * P * D_RF * D_BB
@@ -44,27 +52,27 @@ def tile_gnn_layer_pb_kernel(tc, BB_feature, RF_feature, W_bbbb, b_bbbb, W_rfbb,
             nc.sync.dma_start(out=raw[:, :cols].rearrange("p (j k) -> p j k", j=row_tiles), in_=view)
             return raw
 
-        def x_view(q):
-            return BB_feature[:, q * CHUNK : (q + 1) * CHUNK, :]
+        def load_x(chunk):
+            return load(BB_feature[:, chunk * CHUNK : (chunk + 1) * CHUNK, :], CHUNK)
 
-        def w_view(weight, first_row, row_tiles):
-            return weight[first_row : first_row + row_tiles * P, :].rearrange("(j p) k -> p j k", p=P)
+        def load_weight(weight, batch, row_tiles):
+            rows = weight[batch * row_tiles * P : (batch + 1) * row_tiles * P, :]
+            return load(rows.rearrange("(j p) k -> p j k", p=P), row_tiles)
 
-        raw_wbb0 = load(w_view(W_bbbb, 0, 4), 4)
-        raw_x0 = load(x_view(0), CHUNK)
+        raw_w_bb = [load_weight(W_bbbb, 0, CHUNK)]
+        raw_x = [load_x(0)]
         bias_rows = const.tile([P, 2 * D_BB], BF16, name="bias_rows")
         nc.vector.memset(bias_rows[:], 0.0)
         nc.sync.dma_start(out=bias_rows[0:1, :D_BB], in_=b_bbbb.rearrange("(o n) -> o n", o=1))
         nc.sync.dma_start(out=bias_rows[0:1, D_BB:], in_=b_rfbb.rearrange("(o n) -> o n", o=1))
-        raw_wbb1 = load(w_view(W_bbbb, HALF, 4), 4)
-        raw_x1 = load(x_view(1), CHUNK)
+        raw_w_bb.append(load_weight(W_bbbb, 1, CHUNK))
+        raw_x.append(load_x(1))
 
         ident = const.tile([P, P], F32, name="ident")
         make_identity(nc, ident[:])
         tiny = const.tile([P, 1], F32, name="tiny")
         nc.vector.memset(tiny[:], TINY)
         warm = const.tile([P, 1], F32, name="warm")
-
         ones = const.tile([P, P], BF16, name="ones")
         nc.vector.memset(ones[:], 1.0)
         bias_bb = const.tile([P, D_BB], BF16, name="bias_bb")
@@ -76,46 +84,45 @@ def tile_gnn_layer_pb_kernel(tc, BB_feature, RF_feature, W_bbbb, b_bbbb, W_rfbb,
         load_sigmoid_table()
 
         def spread_bias(spread, first):
-            for h in range(D_BB // HALF):
-                row = bias_rows[:, first + h * HALF : first + (h + 1) * HALF]
-                acc = acc_psum.tile([P, HALF], F32, name="acc")
+            for h in range(HALVES):
+                acc = acc_psum.tile([P, BANK], F32, name="acc")
+                row = bias_rows[:, first + h * BANK : first + (h + 1) * BANK]
                 nc.tensor.matmul(out=acc[:], lhsT=ones[:], rhs=row, start=True, stop=True)
-                nc.vector.tensor_copy(out=spread[:, h * HALF : (h + 1) * HALF], in_=acc[:])
+                nc.vector.tensor_copy(out=spread[:, h * BANK : (h + 1) * BANK], in_=acc[:])
 
-        z = [work.tile([P, D_BB], F32, name="z%d" % g) for g in range(GROUPS + 1)]
-        w = [work.tile([P, D_BB], F32, name="w%d" % g) for g in range(GROUPS + 1)]
-        RF = GROUPS
+        z = [work.tile([P, D_BB], F32, name="z%d" % i) for i in range(GROUPS + 1)]
+        val = [work.tile([P, D_BB], F32, name="w%d" % i) for i in range(GROUPS + 1)]
 
-        def flip(raw, blocks):
+        def flip(raw, passes, row_tiles):
             words = raw[:].bitcast(F32)
             banks = []
-            for first in range(0, blocks, BLOCKS_PER_BANK):
+            for first in range(0, row_tiles * passes * BLOCKS_PER_PASS, BLOCKS_PER_BANK):
                 bank = flip_psum.tile([P, BLOCKS_PER_BANK, P], F32, name="bank")
                 for s in range(BLOCKS_PER_BANK):
-                    n = first + s
-                    nc.tensor.transpose(bank[:, s, :], words[:, n * P : (n + 1) * P], ident[:])
+                    block = words[:, (first + s) * P : (first + s + 1) * P]
+                    nc.tensor.transpose(bank[:, s, :], block, ident[:])
                 banks.append(bank)
             return banks
 
-        def regroup(banks, passes, row_tiles, scalar_banks):
+        def regroup(banks, passes, row_tiles, scalar_helps):
             grouped = grouped_pool.tile([P, BATCH], BF16, name="grouped", align_bytes=64)
-            cols = passes * row_tiles * P * 4
+            cols = passes * row_tiles * P * PACK
             pairs = grouped[:, :cols].bitcast(F32).rearrange(
-                "p (c j r u) -> p c j r u", c=passes, j=row_tiles, u=2
+                "p (c j r u) -> p c j r u", c=passes, j=row_tiles, u=BLOCKS_PER_PASS
             )
             banks_per_row_tile = passes // 2
             for k, bank in enumerate(banks):
                 j, h = divmod(k, banks_per_row_tile)
                 dst = pairs[:, 2 * h : 2 * h + 2, j]
-                src = bank[:].rearrange("p (c u) r -> p c r u", u=2)
-                if k >= len(banks) - scalar_banks:
+                src = bank[:].rearrange("p (c u) r -> p c r u", u=BLOCKS_PER_PASS)
+                if scalar_helps and k >= len(banks) // 2:
                     nc.scalar.copy(out=dst, in_=src)
                 else:
                     nc.vector.tensor_copy(out=dst, in_=src)
             return grouped[:, :cols]
 
         def quantise(grouped, pool, tag):
-            words = grouped.shape[-1] // 4
+            words = grouped.shape[-1] // PACK
             codes = pool.tile([P, words], U32, name="codes_" + tag, align_bytes=64)
             scales = pool.tile([P, words], U8, name="scales_" + tag, align_bytes=64)
             nc.vector.quantize_mx(out=codes[:].bitcast(FP8X4), scales=scales[:], in_=grouped)
@@ -137,134 +144,136 @@ def tile_gnn_layer_pb_kernel(tc, BB_feature, RF_feature, W_bbbb, b_bbbb, W_rfbb,
                     stop=(c == passes - 1),
                 )
 
-        w_bb = [None, None]
+        w_bb = []
 
         def multiply_bb(x_mx, g, h):
-            acc = acc_psum.tile([P, HALF], F32, name="acc")
-            product(acc[:], x_mx, g % CHUNK, CHUNK, w_bb[h], HALF, D_BB // K_PASS)
-            cols = slice(h * HALF, (h + 1) * HALF)
+            acc = acc_psum.tile([P, BANK], F32, name="acc")
+            product(acc[:], x_mx, g % CHUNK, CHUNK, w_bb[h], BANK, PASSES_BB)
+            cols = slice(h * BANK, (h + 1) * BANK)
             nc.vector.tensor_tensor(out=z[g][:, cols], in0=acc[:], in1=bias_bb[:, cols], op=ALU.add)
 
-        def sigmoid(g, cols=slice(0, D_BB)):
-            nc.scalar.activation(out=w[g][:, cols], in_=z[g][:, cols], func=FUNC.Sigmoid, scale=-1.0)
+        def groups_of(chunk):
+            return range(chunk * CHUNK, (chunk + 1) * CHUNK)
 
-        def log(g):
-            nc.scalar.activation(out=w[g][:], in_=w[g][:], func=FUNC.Ln, bias=tiny[:])
+        def sigmoid(i, cols=slice(0, D_BB)):
+            nc.scalar.activation(out=val[i][:, cols], in_=z[i][:, cols], func=FUNC.Sigmoid, scale=-1.0)
 
-        def tanh(g):
-            nc.scalar.activation(out=w[g][:], in_=w[g][:], func=FUNC.Tanh, scale=-1.0)
+        def log(i):
+            nc.scalar.activation(out=val[i][:], in_=val[i][:], func=FUNC.Ln, bias=tiny[:])
 
-        def times_z(engine, g):
-            engine.tensor_tensor(out=w[g][:], in0=z[g][:], in1=w[g][:], op=ALU.mult)
+        def tanh(i):
+            nc.scalar.activation(out=val[i][:], in_=val[i][:], func=FUNC.Tanh, scale=-1.0)
+
+        def times_z_on_gpsimd(g):
+            nc.gpsimd.tensor_tensor(out=val[g][:], in0=z[g][:], in1=val[g][:], op=ALU.mult)
 
         def park(values, pool, name):
             banks = []
-            for h in range(D_BB // HALF):
-                bank = pool.tile([P, HALF], F32, name=name)
-                nc.tensor.matmul(out=bank[:], lhsT=ident[:], rhs=values[:, h * HALF : (h + 1) * HALF], start=True, stop=True)
+            for h in range(HALVES):
+                bank = pool.tile([P, BANK], F32, name=name)
+                half = values[:, h * BANK : (h + 1) * BANK]
+                nc.tensor.matmul(out=bank[:], lhsT=ident[:], rhs=half, start=True, stop=True)
                 banks.append(bank)
             return banks
 
-        def with_parked(g, banks, op):
-            for h in range(D_BB // HALF):
-                cols = slice(h * HALF, (h + 1) * HALF)
-                nc.vector.tensor_tensor(out=w[g][:, cols], in0=banks[h][:], in1=w[g][:, cols], op=op)
+        def with_parked(i, banks, op):
+            for h in range(HALVES):
+                cols = slice(h * BANK, (h + 1) * BANK)
+                nc.vector.tensor_tensor(out=val[i][:, cols], in0=banks[h][:], in1=val[i][:, cols], op=op)
 
-        def finish(g):
+        def finish(g, rf_banks):
             with_parked(g, rf_banks, ALU.add)
-            nc.sync.dma_start(out=out[:, g, :], in_=w[g][:])
+            nc.sync.dma_start(out=out[:, g, :], in_=val[g][:])
 
-        g_wbb0 = regroup(flip(raw_wbb0, 16), 2, 4, 2)
-        raw_x2 = load(x_view(2), CHUNK)
-        w_bb[0] = quantise(g_wbb0, keep, "wbb0")
-        g_x0 = regroup(flip(raw_x0, 16), 2, CHUNK, 2)
+
+        grouped_w = regroup(flip(raw_w_bb[0], PASSES_BB, CHUNK), PASSES_BB, CHUNK, True)
+        raw_x.append(load_x(2))
+        w_bb.append(quantise(grouped_w, keep, "wbb0"))
+        grouped_x = regroup(flip(raw_x[0], PASSES_BB, CHUNK), PASSES_BB, CHUNK, True)
         raw_rf = load(RF_feature.rearrange("b (j k) -> b j k", j=1), 1)
-        x0 = quantise(g_x0, turn, "turn")
+        x_mx = quantise(grouped_x, turn, "turn")
         spread_bias(bias_bb, 0)
-        g_wbb1 = regroup(flip(raw_wbb1, 16), 2, 4, 4)
-        raw_wrf = [load(w_view(W_rfbb, 0, 2), 2)]
-        for g in range(0, CHUNK // 2):
-            multiply_bb(x0, g, 0)
-            sigmoid(g, slice(0, HALF))
-        w_bb[1] = quantise(g_wbb1, keep, "wbb1")
-        for g in range(CHUNK // 2, CHUNK):
-            multiply_bb(x0, g, 0)
-            sigmoid(g, slice(0, HALF))
-        banks_x1 = flip(raw_x1, 16)
-        raw_wrf.append(load(w_view(W_rfbb, 2 * P, 2), 2))
-        g_x1 = regroup(banks_x1, 2, CHUNK, 4)
-        for g in range(0, CHUNK):
-            multiply_bb(x0, g, 1)
-            sigmoid(g, slice(HALF, D_BB))
-
-        banks_x2 = flip(raw_x2, 16)
-        x1 = quantise(g_x1, turn, "turn")
-        g_x2 = regroup(banks_x2, 2, CHUNK, 2)
-        raw_wrf.append(load(w_view(W_rfbb, 4 * P, 2), 2))
-        for g in range(CHUNK, 2 * CHUNK):
-            multiply_bb(x1, g, 0)
-            multiply_bb(x1, g, 1)
+        grouped_w = regroup(flip(raw_w_bb[1], PASSES_BB, CHUNK), PASSES_BB, CHUNK, True)
+        raw_w_rf = [load_weight(W_rfbb, 0, TILES_W_RF)]
+        for g in groups_of(0):
+            multiply_bb(x_mx, g, 0)
+            sigmoid(g, slice(0, BANK))
+        w_bb.append(quantise(grouped_w, keep, "wbb1"))
+        grouped_x = regroup(flip(raw_x[1], PASSES_BB, CHUNK), PASSES_BB, CHUNK, True)
+        raw_w_rf.append(load_weight(W_rfbb, 1, TILES_W_RF))
+        for g in groups_of(0):
+            multiply_bb(x_mx, g, 1)
+            sigmoid(g, slice(BANK, D_BB))
+        banks_x = flip(raw_x[2], PASSES_BB, CHUNK)
+        x_mx = quantise(grouped_x, turn, "turn")
+        grouped_x = regroup(banks_x, PASSES_BB, CHUNK, True)
+        raw_w_rf.append(load_weight(W_rfbb, 2, TILES_W_RF))
+        for g in groups_of(1):
+            for h in range(HALVES):
+                multiply_bb(x_mx, g, h)
             sigmoid(g)
-        x2 = quantise(g_x2, turn, "turn")
+        x_mx = quantise(grouped_x, turn, "turn")
+
         for g in range(0, 2 * CHUNK):
             log(g)
-
         spread_bias(bias_rf, D_BB)
-        g_rf = regroup(flip(raw_rf, 8), 4, 1, 0)
-        raw_wrf.append(load(w_view(W_rfbb, 6 * P, 2), 2))
-        g_wrf = regroup(flip(raw_wrf[0], 16), 4, 2, 0)
-        raw_x3 = load(x_view(3), CHUNK)
-        for g in range(2 * CHUNK, 3 * CHUNK):
-            multiply_bb(x2, g, 0)
-            multiply_bb(x2, g, 1)
+        grouped_rf = regroup(flip(raw_rf, PASSES_RF, 1), PASSES_RF, 1, False)
+        raw_w_rf.append(load_weight(W_rfbb, 3, TILES_W_RF))
+        grouped_w = regroup(flip(raw_w_rf[0], PASSES_RF, TILES_W_RF), PASSES_RF, TILES_W_RF, False)
+        raw_x.append(load_x(3))
+
+        for g in groups_of(2):
+            for h in range(HALVES):
+                multiply_bb(x_mx, g, h)
             sigmoid(g)
-        rf_mx = quantise(g_rf, keep, "rf")
-        wrf_mx = quantise(g_wrf, turn, "turn")
+        rf_mx = quantise(grouped_rf, keep, "rf")
+        w_rf_mx = quantise(grouped_w, turn, "turn")
         for g in range(0, 2 * CHUNK):
             tanh(g)
-            times_z(nc.gpsimd, g)
+            times_z_on_gpsimd(g)
 
-        WIDTH_RF = 2 * P
-        for i in range(4):
-            if i < 3:
-                g_next = regroup(flip(raw_wrf[i + 1], 16), 4, 2, 0)
-            acc = acc_psum.tile([P, HALF], F32, name="acc")
-            product(acc[:, :WIDTH_RF], rf_mx, 0, 1, wrf_mx, WIDTH_RF, D_RF // K_PASS)
-            cols = slice(i * WIDTH_RF, (i + 1) * WIDTH_RF)
-            nc.vector.tensor_tensor(out=z[RF][:, cols], in0=acc[:, :WIDTH_RF], in1=bias_rf[:, cols], op=ALU.add)
-            if i < 3:
-                wrf_mx = quantise(g_next, turn, "turn")
+        width = TILES_W_RF * P
+        for i in range(BATCHES_W_RF):
+            if i + 1 < BATCHES_W_RF:
+                grouped_w = regroup(flip(raw_w_rf[i + 1], PASSES_RF, TILES_W_RF), PASSES_RF, TILES_W_RF, False)
+            acc = acc_psum.tile([P, BANK], F32, name="acc")
+            product(acc[:, :width], rf_mx, 0, 1, w_rf_mx, width, PASSES_RF)
+            cols = slice(i * width, (i + 1) * width)
+            nc.vector.tensor_tensor(out=z[RF][:, cols], in0=acc[:, :width], in1=bias_rf[:, cols], op=ALU.add)
+            if i + 1 < BATCHES_W_RF:
+                w_rf_mx = quantise(grouped_w, turn, "turn")
         sigmoid(RF)
         z_rf_banks = park(z[RF], flip_psum, "bank")
-        x3 = quantise(regroup(flip(raw_x3, 16), 2, CHUNK, 0), turn, "turn")
 
+        x_mx = quantise(regroup(flip(raw_x[3], PASSES_BB, CHUNK), PASSES_BB, CHUNK, False), turn, "turn")
         log(RF)
-        for g in range(2 * CHUNK, 3 * CHUNK):
+        for g in groups_of(2):
             log(g)
-        for g in range(3 * CHUNK, GROUPS):
-            multiply_bb(x3, g, 0)
-            multiply_bb(x3, g, 1)
+        for g in groups_of(3):
+            for h in range(HALVES):
+                multiply_bb(x_mx, g, h)
 
         load_sigmoid_table()
         tanh(RF)
         with_parked(RF, z_rf_banks, ALU.mult)
-        rf_banks = park(w[RF], flip_psum, "bank")
+        rf_banks = park(val[RF], flip_psum, "bank")
         for g in range(0, 2 * CHUNK):
-            finish(g)
-        for g in range(3 * CHUNK, GROUPS):
+            finish(g, rf_banks)
+        for g in groups_of(3):
             sigmoid(g)
+        for g in groups_of(2):
+            tanh(g)
+            times_z_on_gpsimd(g)
+            finish(g, rf_banks)
 
-        for g in range(2 * CHUNK, 3 * CHUNK):
-            tanh(g)
-            times_z(nc.gpsimd, g)
-            finish(g)
-        for g in range(3 * CHUNK, GROUPS):
+        for g in groups_of(3):
             log(g)
-        z_banks = [park(z[g], acc_psum, "acc") for g in range(3 * CHUNK + 1, GROUPS, 2)]
-        for g in range(3 * CHUNK, GROUPS, 2):
+        odd = range(3 * CHUNK + 1, GROUPS, 2)
+        z_banks = [park(z[g], acc_psum, "acc") for g in odd]
+        for g, banks in zip(odd, z_banks):
+            tanh(g - 1)
+            times_z_on_gpsimd(g - 1)
             tanh(g)
-            times_z(nc.gpsimd, g)
-            tanh(g + 1)
-            with_parked(g + 1, z_banks[(g - 3 * CHUNK) // 2], ALU.mult)
-            finish(g + 1)
-            finish(g)
+            with_parked(g, banks, ALU.mult)
+            finish(g, rf_banks)
+            finish(g - 1, rf_banks)

from contextlib import ExitStack

import concourse.mybir as mybir
from concourse.masks import make_identity

F32 = mybir.dt.float32
BF16 = mybir.dt.bfloat16
U32 = mybir.dt.uint32
U8 = mybir.dt.uint8
FP8X4 = mybir.dt.float8_e4m3fn_x4
FUNC = mybir.ActivationFunctionType
ALU = mybir.AluOpType

P = 128
GROUPS = 16
D_BB = 1024
D_RF = 2048
PACK = 4
K_PASS = P * PACK
PASSES_BB = D_BB // K_PASS
PASSES_RF = D_RF // K_PASS
BANK = 512
HALVES = D_BB // BANK
BLOCKS_PER_BANK = BANK // P
BLOCKS_PER_PASS = 2
BATCH = 4096
CHUNK = BATCH // D_BB
TILES_W_RF = BATCH // D_RF
BATCHES_W_RF = D_BB // (TILES_W_RF * P)
RF = GROUPS
TINY = 2.0 ** -60

FLOPS = 2 * P * GROUPS * D_BB * D_BB + 2 * P * D_RF * D_BB


def tile_gnn_layer_pb_kernel(tc, BB_feature, RF_feature, W_bbbb, b_bbbb, W_rfbb, b_rfbb, out):
    nc = tc.nc
    with ExitStack() as stack:
        const = stack.enter_context(tc.tile_pool(name="const", bufs=1))
        raw_pool = stack.enter_context(tc.tile_pool(name="raw", bufs=4))
        grouped_pool = stack.enter_context(tc.tile_pool(name="grouped", bufs=3))
        keep = stack.enter_context(tc.tile_pool(name="keep", bufs=1))
        turn = stack.enter_context(tc.tile_pool(name="turn", bufs=3))
        work = stack.enter_context(tc.tile_pool(name="work", bufs=1))
        flip_psum = stack.enter_context(tc.psum_pool(name="flip", bufs=4))
        acc_psum = stack.enter_context(tc.psum_pool(name="acc", bufs=4))
        stack.enter_context(tc.manual_schedule())

        def load(view, row_tiles):
            raw = raw_pool.tile([P, BATCH], BF16, name="raw")
            cols = view.shape[-1] * row_tiles
            nc.sync.dma_start(out=raw[:, :cols].rearrange("p (j k) -> p j k", j=row_tiles), in_=view)
            return raw

        def load_x(chunk):
            return load(BB_feature[:, chunk * CHUNK : (chunk + 1) * CHUNK, :], CHUNK)

        def load_weight(weight, batch, row_tiles):
            rows = weight[batch * row_tiles * P : (batch + 1) * row_tiles * P, :]
            return load(rows.rearrange("(j p) k -> p j k", p=P), row_tiles)

        raw_w_bb = [load_weight(W_bbbb, 0, CHUNK)]
        raw_x = [load_x(0)]
        bias_rows = const.tile([P, 2 * D_BB], BF16, name="bias_rows")
        nc.vector.memset(bias_rows[:], 0.0)
        nc.sync.dma_start(out=bias_rows[0:1, :D_BB], in_=b_bbbb.rearrange("(o n) -> o n", o=1))
        nc.sync.dma_start(out=bias_rows[0:1, D_BB:], in_=b_rfbb.rearrange("(o n) -> o n", o=1))
        raw_w_bb.append(load_weight(W_bbbb, 1, CHUNK))
        raw_x.append(load_x(1))

        ident = const.tile([P, P], F32, name="ident")
        make_identity(nc, ident[:])
        tiny = const.tile([P, 1], F32, name="tiny")
        nc.vector.memset(tiny[:], TINY)
        warm = const.tile([P, 1], F32, name="warm")
        ones = const.tile([P, P], BF16, name="ones")
        nc.vector.memset(ones[:], 1.0)
        bias_bb = const.tile([P, D_BB], BF16, name="bias_bb")
        bias_rf = const.tile([P, D_BB], BF16, name="bias_rf")

        def load_sigmoid_table():
            nc.scalar.activation(out=warm[:], in_=tiny[:], func=FUNC.Sigmoid)

        load_sigmoid_table()

        def spread_bias(spread, first):
            for h in range(HALVES):
                acc = acc_psum.tile([P, BANK], F32, name="acc")
                row = bias_rows[:, first + h * BANK : first + (h + 1) * BANK]
                nc.tensor.matmul(out=acc[:], lhsT=ones[:], rhs=row, start=True, stop=True)
                nc.vector.tensor_copy(out=spread[:, h * BANK : (h + 1) * BANK], in_=acc[:])

        z = [work.tile([P, D_BB], F32, name="z%d" % i) for i in range(GROUPS + 1)]
        val = [work.tile([P, D_BB], F32, name="w%d" % i) for i in range(GROUPS + 1)]

        def flip(raw, passes, row_tiles):
            words = raw[:].bitcast(F32)
            banks = []
            for first in range(0, row_tiles * passes * BLOCKS_PER_PASS, BLOCKS_PER_BANK):
                bank = flip_psum.tile([P, BLOCKS_PER_BANK, P], F32, name="bank")
                for s in range(BLOCKS_PER_BANK):
                    block = words[:, (first + s) * P : (first + s + 1) * P]
                    nc.tensor.transpose(bank[:, s, :], block, ident[:])
                banks.append(bank)
            return banks

        def regroup(banks, passes, row_tiles, scalar_helps):
            grouped = grouped_pool.tile([P, BATCH], BF16, name="grouped", align_bytes=64)
            cols = passes * row_tiles * P * PACK
            pairs = grouped[:, :cols].bitcast(F32).rearrange(
                "p (c j r u) -> p c j r u", c=passes, j=row_tiles, u=BLOCKS_PER_PASS
            )
            banks_per_row_tile = passes // 2
            for k, bank in enumerate(banks):
                j, h = divmod(k, banks_per_row_tile)
                dst = pairs[:, 2 * h : 2 * h + 2, j]
                src = bank[:].rearrange("p (c u) r -> p c r u", u=BLOCKS_PER_PASS)
                if scalar_helps and k >= len(banks) // 2:
                    nc.scalar.copy(out=dst, in_=src)
                else:
                    nc.vector.tensor_copy(out=dst, in_=src)
            return grouped[:, :cols]

        def quantise(grouped, pool, tag):
            words = grouped.shape[-1] // PACK
            codes = pool.tile([P, words], U32, name="codes_" + tag, align_bytes=64)
            scales = pool.tile([P, words], U8, name="scales_" + tag, align_bytes=64)
            nc.vector.quantize_mx(out=codes[:].bitcast(FP8X4), scales=scales[:], in_=grouped)
            return codes, scales

        def product(acc, stationary, j, row_tiles, moving, width, passes):
            s_codes, s_scales = stationary
            m_codes, m_scales = moving
            for c in range(passes):
                s_cols = slice((c * row_tiles + j) * P, (c * row_tiles + j + 1) * P)
                m_cols = slice(c * width, (c + 1) * width)
                nc.tensor.matmul_mx(
                    out=acc,
                    lhsT=s_codes[:, s_cols].bitcast(FP8X4),
                    lhsT_scale=s_scales[:, s_cols],
                    rhs=m_codes[:, m_cols].bitcast(FP8X4),
                    rhs_scale=m_scales[:, m_cols],
                    start=(c == 0),
                    stop=(c == passes - 1),
                )

        w_bb = []

        def multiply_bb(x_mx, g, h):
            acc = acc_psum.tile([P, BANK], F32, name="acc")
            product(acc[:], x_mx, g % CHUNK, CHUNK, w_bb[h], BANK, PASSES_BB)
            cols = slice(h * BANK, (h + 1) * BANK)
            nc.vector.tensor_tensor(out=z[g][:, cols], in0=acc[:], in1=bias_bb[:, cols], op=ALU.add)

        def groups_of(chunk):
            return range(chunk * CHUNK, (chunk + 1) * CHUNK)

        def sigmoid(i, cols=slice(0, D_BB)):
            nc.scalar.activation(out=val[i][:, cols], in_=z[i][:, cols], func=FUNC.Sigmoid, scale=-1.0)

        def log(i):
            nc.scalar.activation(out=val[i][:], in_=val[i][:], func=FUNC.Ln, bias=tiny[:])

        def tanh(i):
            nc.scalar.activation(out=val[i][:], in_=val[i][:], func=FUNC.Tanh, scale=-1.0)

        def times_z_on_gpsimd(g):
            nc.gpsimd.tensor_tensor(out=val[g][:], in0=z[g][:], in1=val[g][:], op=ALU.mult)

        def park(values, pool, name):
            banks = []
            for h in range(HALVES):
                bank = pool.tile([P, BANK], F32, name=name)
                half = values[:, h * BANK : (h + 1) * BANK]
                nc.tensor.matmul(out=bank[:], lhsT=ident[:], rhs=half, start=True, stop=True)
                banks.append(bank)
            return banks

        def with_parked(i, banks, op):
            for h in range(HALVES):
                cols = slice(h * BANK, (h + 1) * BANK)
                nc.vector.tensor_tensor(out=val[i][:, cols], in0=banks[h][:], in1=val[i][:, cols], op=op)

        def finish(g, rf_banks):
            with_parked(g, rf_banks, ALU.add)
            nc.sync.dma_start(out=out[:, g, :], in_=val[g][:])


        grouped_w = regroup(flip(raw_w_bb[0], PASSES_BB, CHUNK), PASSES_BB, CHUNK, True)
        raw_x.append(load_x(2))
        w_bb.append(quantise(grouped_w, keep, "wbb0"))
        grouped_x = regroup(flip(raw_x[0], PASSES_BB, CHUNK), PASSES_BB, CHUNK, True)
        raw_rf = load(RF_feature.rearrange("b (j k) -> b j k", j=1), 1)
        x_mx = quantise(grouped_x, turn, "turn")
        spread_bias(bias_bb, 0)
        grouped_w = regroup(flip(raw_w_bb[1], PASSES_BB, CHUNK), PASSES_BB, CHUNK, True)
        raw_w_rf = [load_weight(W_rfbb, 0, TILES_W_RF)]
        for g in groups_of(0):
            multiply_bb(x_mx, g, 0)
            sigmoid(g, slice(0, BANK))
        w_bb.append(quantise(grouped_w, keep, "wbb1"))
        grouped_x = regroup(flip(raw_x[1], PASSES_BB, CHUNK), PASSES_BB, CHUNK, True)
        raw_w_rf.append(load_weight(W_rfbb, 1, TILES_W_RF))
        for g in groups_of(0):
            multiply_bb(x_mx, g, 1)
            sigmoid(g, slice(BANK, D_BB))
        banks_x = flip(raw_x[2], PASSES_BB, CHUNK)
        x_mx = quantise(grouped_x, turn, "turn")
        grouped_x = regroup(banks_x, PASSES_BB, CHUNK, True)
        raw_w_rf.append(load_weight(W_rfbb, 2, TILES_W_RF))
        for g in groups_of(1):
            for h in range(HALVES):
                multiply_bb(x_mx, g, h)
            sigmoid(g)
        x_mx = quantise(grouped_x, turn, "turn")

        for g in range(0, 2 * CHUNK):
            log(g)
        spread_bias(bias_rf, D_BB)
        grouped_rf = regroup(flip(raw_rf, PASSES_RF, 1), PASSES_RF, 1, False)
        raw_w_rf.append(load_weight(W_rfbb, 3, TILES_W_RF))
        grouped_w = regroup(flip(raw_w_rf[0], PASSES_RF, TILES_W_RF), PASSES_RF, TILES_W_RF, False)
        raw_x.append(load_x(3))

        for g in groups_of(2):
            for h in range(HALVES):
                multiply_bb(x_mx, g, h)
            sigmoid(g)
        rf_mx = quantise(grouped_rf, keep, "rf")
        w_rf_mx = quantise(grouped_w, turn, "turn")
        for g in range(0, 2 * CHUNK):
            tanh(g)
            times_z_on_gpsimd(g)

        width = TILES_W_RF * P
        for i in range(BATCHES_W_RF):
            if i + 1 < BATCHES_W_RF:
                grouped_w = regroup(flip(raw_w_rf[i + 1], PASSES_RF, TILES_W_RF), PASSES_RF, TILES_W_RF, False)
            acc = acc_psum.tile([P, BANK], F32, name="acc")
            product(acc[:, :width], rf_mx, 0, 1, w_rf_mx, width, PASSES_RF)
            cols = slice(i * width, (i + 1) * width)
            nc.vector.tensor_tensor(out=z[RF][:, cols], in0=acc[:, :width], in1=bias_rf[:, cols], op=ALU.add)
            if i + 1 < BATCHES_W_RF:
                w_rf_mx = quantise(grouped_w, turn, "turn")
        sigmoid(RF)
        z_rf_banks = park(z[RF], flip_psum, "bank")

        x_mx = quantise(regroup(flip(raw_x[3], PASSES_BB, CHUNK), PASSES_BB, CHUNK, False), turn, "turn")
        log(RF)
        for g in groups_of(2):
            log(g)
        for g in groups_of(3):
            for h in range(HALVES):
                multiply_bb(x_mx, g, h)

        load_sigmoid_table()
        tanh(RF)
        with_parked(RF, z_rf_banks, ALU.mult)
        rf_banks = park(val[RF], flip_psum, "bank")
        for g in range(0, 2 * CHUNK):
            finish(g, rf_banks)
        for g in groups_of(3):
            sigmoid(g)
        for g in groups_of(2):
            tanh(g)
            times_z_on_gpsimd(g)
            finish(g, rf_banks)

        for g in groups_of(3):
            log(g)
        odd = range(3 * CHUNK + 1, GROUPS, 2)
        z_banks = [park(z[g], acc_psum, "acc") for g in odd]
        for g, banks in zip(odd, z_banks):
            tanh(g - 1)
            times_z_on_gpsimd(g - 1)
            tanh(g)
            with_parked(g, banks, ALU.mult)
            finish(g, rf_banks)
            finish(g - 1, rf_banks)
